import numpy as np
import ml_dtypes


def mxq(x, axis, fmt="e4m3"):
    dtype, down = {"e4m3": (ml_dtypes.float8_e4m3fn, 7), "e5m2": (ml_dtypes.float8_e5m2, 14)}[fmt]
    v = np.moveaxis(np.asarray(x, np.float32).astype(ml_dtypes.bfloat16).astype(np.float64), axis, -1)
    blocks = v.reshape(v.shape[:-1] + (-1, 32))
    amax = np.abs(blocks).max(-1, keepdims=True)
    byte = np.maximum(np.where(amax > 0, np.frexp(amax)[1] - 1 + 127, 0) - down, 1)
    scale = np.exp2(byte - 127.0)
    codes = (blocks / scale).astype(np.float32).astype(dtype).astype(np.float64)
    return np.moveaxis((codes * scale).reshape(v.shape), -1, axis)


WIDE = False


def mx_kscale(k):
    if not WIDE:
        return np.ones(k)
    levels = np.array([18, -18])
    if k % 512:
        return np.exp2(np.random.permutation(np.resize(levels, k // 32))).repeat(32)
    a = np.empty((k // 512, 16))
    for p in range(k // 512):
        a[p, :8] = np.random.permutation(np.resize(levels, 8))
        for g in range(8):
            far = levels[np.abs(levels - a[p, g]) >= 10]
            a[p, g + 8] = far[np.random.randint(len(far))]
    return np.exp2(a.ravel()).repeat(32)


BF16 = ml_dtypes.bfloat16


def bf(x):
    return np.asarray(x, np.float32).astype(BF16)


def f64(x):
    return np.asarray(x).astype(np.float64)


B, L, D, H, P = 2, 256, 1024, 4, 512
HD = D // H
HH = HD // 2
LT = L + P
T = P + B * L


def rotate_half_back(t):
    return np.concatenate([t[..., HH:], -t[..., :HH]], axis=-1)


def unrotate(g, cos, sin):
    return g * cos[None, :, None, :] + rotate_half_back(g * sin[None, :, None, :])


def pair_scale():
    h = mx_kscale(H * HH).reshape(H, HH)
    return np.concatenate([h, h], axis=1).reshape(D)


def setup_inputs():
    s = mx_kscale(T)
    sm = s[:P]
    sx = s[P:].reshape(B, L)
    st = np.concatenate([np.broadcast_to(sm, (B, P)), sx], axis=1).reshape(B, LT, 1, 1)
    uq = pair_scale()
    uk = pair_scale()
    uv = mx_kscale(D)
    x = bf(np.random.standard_normal((B, L, D)) * sx[:, :, None])
    pmem = bf(np.random.standard_normal((1, P, D)) * sm[None, :, None])
    cos = bf(np.random.uniform(size=(LT, HD)))
    sin = bf(np.random.uniform(size=(LT, HD)))
    wq = bf(np.random.standard_normal((D, D)) / np.sqrt(D) / uq)
    wk = bf(np.random.standard_normal((D, D)) / np.sqrt(D) / uk)
    wv = bf(np.random.standard_normal((D, D)) / np.sqrt(D) / uv)
    gs = []
    for u in (uq, uk, uv):
        e = np.exp2(np.random.randint(-6, 1, (B, LT, 1, 1)))
        gs.append(bf(np.random.standard_normal((B, LT, H, HD)) * e / st * u.reshape(H, HD)))
    return {"x": x, "pmem": pmem, "cos": cos, "sin": sin, "wq": wq, "wk": wk, "wv": wv,
            "grad_0": gs[0], "grad_1": gs[1], "grad_2": gs[2]}


def reference(x, pmem, cos, sin, wq, wk, wv, grad_0, grad_1, grad_2):
    cc = f64(cos)
    ss = f64(sin)
    dq = unrotate(f64(grad_0), cc, ss).reshape(B, LT, D)
    dk = unrotate(f64(grad_1), cc, ss).reshape(B, LT, D)
    dv = f64(grad_2).reshape(B, LT, D)
    dz = np.concatenate([dq, dk, dv], axis=2)
    dz_x = dz[:, P:].reshape(B * L, 3 * D)
    dz_m = dz[:, :P].sum(axis=0)
    dz_t = np.concatenate([dz_m, dz_x], axis=0)
    x_t = np.concatenate([f64(pmem)[0], f64(x).reshape(B * L, D)], axis=0)
    w = np.concatenate([f64(wq), f64(wk), f64(wv)], axis=1)
    dx = mxq(dz_x, 1, "e5m2") @ mxq(w, 1, "e4m3").T
    dw = mxq(x_t, 0, "e4m3").T @ mxq(dz_t, 0, "e5m2")
    return dx.reshape(B, L, D), dw[:, :D], dw[:, D:2 * D], dw[:, 2 * D:]

from contextlib import ExitStack

import concourse.mybir as mybir
from concourse.masks import make_identity

B, L, D, H, PM = 2, 256, 1024, 4, 512
HD = D // H
FLOPS = 2 * (B * L) * (3 * D) * D + 2 * D * (PM + B * L) * (3 * D)

F32 = mybir.dt.float32
BF16 = mybir.dt.bfloat16
U32 = mybir.dt.uint32
U8 = mybir.dt.uint8
E4M3 = mybir.dt.float8_e4m3fn_x4
E5M2 = mybir.dt.float8_e5m2_x4
MULT = mybir.AluOpType.mult
ADD = mybir.AluOpType.add

P = 128
NT = 512


def tile_titanstnt_pa_v_kernel(
    tc, x, pmem, cos, sin, wq, wk, wv, grad_0, grad_1, grad_2, out_0, out_1, out_2, out_3
):
    nc = tc.nc
    grads = (grad_0, grad_1, grad_2)
    weights = (wq, wk, wv)
    douts = (out_1, out_2, out_3)

    with ExitStack() as ctx:
        keep = ctx.enter_context(tc.tile_pool(name="keep", bufs=1))
        rx = ctx.enter_context(tc.tile_pool(name="rx", bufs=3))
        raw = ctx.enter_context(tc.tile_pool(name="raw", bufs=6))
        prod = ctx.enter_context(tc.tile_pool(name="prod", bufs=2))
        dzp = ctx.enter_context(tc.tile_pool(name="dzp", bufs=4))
        stg = ctx.enter_context(tc.tile_pool(name="stg", bufs=6))
        outp = ctx.enter_context(tc.tile_pool(name="outp", bufs=3))
        ps_s = ctx.enter_context(tc.psum_pool(name="ps_s", bufs=4))
        ps_b = ctx.enter_context(tc.psum_pool(name="ps_b", bufs=4))
        ctx.enter_context(tc.manual_schedule())

        id_f = keep.tile([P, P], F32, name="id_f")
        make_identity(nc, id_f[:])
        id_b = keep.tile([P, P], BF16, name="id_b")
        nc.vector.tensor_copy(out=id_b[:], in_=id_f[:])

        cos_m = keep.tile([P, 4, HD], BF16, name="cos_m")
        sin_m = keep.tile([P, 4, HD], BF16, name="sin_m")
        cos_x = keep.tile([P, 4, HD], BF16, name="cos_x")
        sin_x = keep.tile([P, 4, HD], BF16, name="sin_x")
        x_codes = keep.tile([P, 2, D], U32, name="x_codes", align_bytes=64)
        x_scales = keep.tile([P, 2, D], U8, name="x_scales", align_bytes=64)
        t_codes = keep.tile([P, 6, NT], U32, name="t_codes", align_bytes=64)
        t_scales = keep.tile([P, 6, NT], U8, name="t_scales", align_bytes=64)
        w_codes = keep.tile([P, 6, D], U32, name="w_codes", align_bytes=64)
        w_scales = keep.tile([P, 6, D], U8, name="w_scales", align_bytes=64)
        z_codes = keep.tile([P, 3, 2, D], U32, name="z_codes", align_bytes=64)
        z_scales = keep.tile([P, 3, 2, D], U8, name="z_scales", align_bytes=64)

        gm = {}
        gx = {}
        xr = {}
        w_raw = {}
        st = {}
        prods = {}
        sums = {}

        def load_gm(i, b):
            t = raw.tile([P, 4, D], BF16, name="raw")
            nc.sync.dma_start(out=t[:], in_=grads[i][b, 0:PM, :, :].rearrange("(p j) h f -> p j (h f)", j=4))
            gm[i, b] = t

        def load_gx(i, h0, h1):
            if i not in gx:
                gx[i] = rx.tile([P, 4, D], BF16, name="rx")
            for b, queue in enumerate((nc.sync, nc.scalar)):
                queue.dma_start(
                    out=gx[i][64 * b : 64 * b + 64, :, h0 * HD : h1 * HD],
                    in_=grads[i][b, PM : PM + L, h0:h1, :].rearrange("(p j) h f -> p j (h f)", j=4),
                )

        def load_x(ps):
            rows = (pmem.rearrange("o t d -> (o t) d"), x.rearrange("b t d -> (b t) d"))[ps]
            t = raw.tile([P, 4, D], BF16, name="raw")
            nc.sync.dma_start(out=t[:], in_=rows.rearrange("(p j) d -> p j d", j=4))
            xr[ps] = t

        def load_w(i, n):
            t = raw.tile([P, 4, D], BF16, name="raw")
            nc.sync.dma_start(
                out=t[:], in_=weights[i][n * NT : (n + 1) * NT, :].rearrange("(b p) o -> p b o", p=P)
            )
            w_raw[i, n] = t

        def load_cs_x():
            for t, src in ((cos_x, cos), (sin_x, sin)):
                for b, queue in enumerate((nc.sync, nc.scalar)):
                    queue.dma_start(
                        out=t[64 * b : 64 * b + 64, :, :],
                        in_=src[PM : PM + L, :].rearrange("(p j) f -> p j f", j=4),
                    )

        def load_cs_m():
            nc.sync.dma_start(out=cos_m[:], in_=cos[0:PM, :].rearrange("(p j) f -> p j f", j=4))
            nc.sync.dma_start(out=sin_m[:], in_=sin[0:PM, :].rearrange("(p j) f -> p j f", j=4))

        def quant(codes, scales, key, fmt):
            nc.vector.quantize_mx(out=codes.bitcast(fmt), scales=scales, in_=st.pop(key)[:])

        def stage(key):
            if key not in st:
                st[key] = stg.tile([P, 4 * NT], BF16, name="stage", align_bytes=64)
            return st[key]

        def interleave(key, src, engine):
            o = stage(key)[:].rearrange("p (c i j) -> p c j i", i=4, j=4)
            s = src.rearrange("p j (c i) -> p c j i", i=4)
            if engine == "g":
                nc.gpsimd.tensor_scalar(out=o, in0=s, scalar1=1.0, scalar2=1.0, op0=MULT, op1=MULT)
            elif engine == "s":
                nc.scalar.copy(out=o, in_=s)
            else:
                nc.vector.tensor_copy(out=o, in_=s)

        def cols(n):
            return slice(n * NT, (n + 1) * NT)

        def mem_sum(pool, name, i, h, s):
            bank = pool.tile([P, 4, P], F32, name=name)
            c0 = h * HD + s * P
            for b in range(B):
                nc.tensor.matmul(
                    out=bank[:], lhsT=id_b[:], rhs=gm[i, b][:, :, c0 : c0 + P], start=(b == 0), stop=(b == B - 1)
                )
            return bank

        def sum_m(i, h):
            for s in range(2):
                sums[i, h, s] = mem_sum(ps_s, "sum_bank", i, h, s)

        def mul_m(i, h):
            a = prod.tile([P, 4, HD], F32, name="prod_a")
            r = prod.tile([P, 4, HD], F32, name="prod_r")
            for s in range(2):
                bank = sums.pop((i, h, s))
                lo = slice(s * P, (s + 1) * P)
                hi = slice((1 - s) * P, (2 - s) * P)
                nc.vector.tensor_tensor(out=a[:, :, lo], in0=bank[:], in1=cos_m[:, :, lo], op=MULT)
                if s == 1:
                    nc.vector.tensor_tensor(out=r[:, :, hi], in0=bank[:], in1=sin_m[:, :, lo], op=MULT)
                else:
                    nc.vector.scalar_tensor_tensor(
                        out=r[:, :, hi], in0=bank[:], scalar=-1.0, in1=sin_m[:, :, lo], op0=MULT, op1=MULT
                    )
            prods["m", i, h] = a, r

        def mul_x(i, h):
            a = prod.tile([P, 4, HD], F32, name="prod_a")
            r = prod.tile([P, 4, HD], F32, name="prod_r")
            g = gx[i][:, :, h * HD : (h + 1) * HD]
            nc.vector.tensor_tensor(out=a[:], in0=g, in1=cos_x[:], op=MULT)
            nc.vector.tensor_tensor(out=r[:, :, 0:P], in0=g[:, :, P:HD], in1=sin_x[:, :, P:HD], op=MULT)
            nc.vector.scalar_tensor_tensor(
                out=r[:, :, P:HD], in0=g[:, :, 0:P], scalar=-1.0, in1=sin_x[:, :, 0:P], op0=MULT, op1=MULT
            )
            prods["x", i, h] = a, r

        def add_m(i, h):
            a, r = prods.pop(("m", i, h))
            k = h % 2
            o = stage(("m", i, h // 2))[:, k * 4 * HD : (k + 1) * 4 * HD]
            nc.vector.tensor_tensor(
                out=o.rearrange("p (c i j) -> p c j i", i=4, j=4),
                in0=a[:].rearrange("p j (c i) -> p c j i", i=4),
                in1=r[:].rearrange("p j (c i) -> p c j i", i=4),
                op=ADD,
            )

        dzx = {}

        def add_x(i, h):
            a, r = prods.pop(("x", i, h))
            n, k = divmod(h, 2)
            if (i, n) not in dzx:
                dzx[i, n] = dzp.tile([P, 4, NT], BF16, name="dzx")
            nc.vector.tensor_tensor(out=dzx[i, n][:, :, k * HD : (k + 1) * HD], in0=a[:], in1=r[:], op=ADD)

        def dz_x(i, n):
            return gx[2][:, :, cols(n)] if i == 2 else dzx[i, n][:]

        def transposed(key, blocks):
            words = stage(key)[:].bitcast(F32).rearrange("f (b r u) -> f b r u", b=4, u=2)
            for pair in range(2):
                bank = ps_b.tile([P, 2, 2, P], F32, name="bank")
                for k in range(2):
                    for u in range(2):
                        nc.tensor.transpose(bank[:, k, u, :], blocks[2 * pair + k][:, u : 256 : 2], id_f[:])
                nc.scalar.copy(
                    out=words[:, 2 * pair : 2 * pair + 2, :, :], in_=bank[:].rearrange("f b u r -> f b r u")
                )

        def t_z(i, n):
            words = (gx[2] if i == 2 else dzx[i, n])[:].bitcast(F32)
            w0 = 256 * n if i == 2 else 0
            transposed(("tz", i, n), [words[:, j, w0 : w0 + 256] for j in range(4)])

        def q_tz(i, n):
            quant(t_codes[:, 2 * i + n, :], t_scales[:, 2 * i + n, :], ("tz", i, n), E5M2)

        def t_w(i, n, g):
            words = w_raw[i, n][:].bitcast(F32)
            transposed(("tw", i, n, g), [words[:, b, 256 * g : 256 * g + 256] for b in range(4)])

        def q_tw(i, n, g):
            quant(w_codes[:, 2 * i + g, cols(n)], w_scales[:, 2 * i + g, cols(n)], ("tw", i, n, g), E4M3)

        def il_x(ps, n, engine):
            interleave(("x", ps, n), xr[ps][:, :, cols(n)], engine)

        def q_x(ps, n):
            quant(x_codes[:, ps, cols(n)], x_scales[:, ps, cols(n)], ("x", ps, n), E4M3)

        def il_z(i, n, engine):
            interleave(("z", i, n), dz_x(i, n), engine)

        def q_z(i, n):
            quant(z_codes[:, i, 1, cols(n)], z_scales[:, i, 1, cols(n)], ("z", i, n), E5M2)

        def v_m(n):
            view = stage(("m", 2, n))[:].rearrange("p (w j) -> p w j", j=4)
            for k in range(4):
                bank = mem_sum(ps_b, "bank", 2, 2 * n + k // 2, k % 2)
                nc.scalar.copy(out=view[:, k * P : (k + 1) * P, :], in_=bank[:].rearrange("p j w -> p w j"))

        def q_m(i, n):
            quant(z_codes[:, i, 0, cols(n)], z_scales[:, i, 0, cols(n)], ("m", i, n), E5M2)

        def evac(engine, out, bank):
            if engine == "s":
                nc.scalar.copy(out=out, in_=bank)
            else:
                nc.vector.tensor_copy(out=out, in_=bank)

        def dw(i, n, mp, engines):
            o = outp.tile([P, 2, NT], F32, name="out_stage")
            for k in range(2):
                m = slice((2 * mp + k) * P, (2 * mp + k + 1) * P)
                bank = ps_b.tile([P, NT], F32, name="bank")
                for ps in range(2):
                    nc.tensor.matmul_mx(
                        out=bank[:],
                        lhsT=x_codes[:, ps, m].bitcast(E4M3), lhsT_scale=x_scales[:, ps, m],
                        rhs=z_codes[:, i, ps, cols(n)].bitcast(E5M2), rhs_scale=z_scales[:, i, ps, cols(n)],
                        start=(ps == 0), stop=(ps == 1),
                    )
                evac(engines[k], o[:, k, :], bank[:])
            nc.sync.dma_start(
                out=douts[i][2 * mp * P : (2 * mp + 2) * P, cols(n)].rearrange("(m p) o -> p m o", p=P), in_=o[:]
            )

        dx_rows = out_0.rearrange("b t d -> (b t) d").rearrange("(p j) d -> p j d", j=4)
        dx_st = {}

        def dx(j, n, engine):
            if j not in dx_st:
                dx_st[j] = outp.tile([P, 2, NT], F32, name="out_stage")
            m = slice(j * P, (j + 1) * P)
            bank = ps_b.tile([P, NT], F32, name="bank")
            for ps in range(6):
                nc.tensor.matmul_mx(
                    out=bank[:],
                    lhsT=t_codes[:, ps, m].bitcast(E5M2), lhsT_scale=t_scales[:, ps, m],
                    rhs=w_codes[:, ps, cols(n)].bitcast(E4M3), rhs_scale=w_scales[:, ps, cols(n)],
                    start=(ps == 0), stop=(ps == 5),
                )
            evac(engine, dx_st[j][:, n, :], bank[:])
            if n == 1:
                nc.sync.dma_start(out=dx_rows[:, j, :], in_=dx_st[j][:].rearrange("p n o -> p (n o)"))

        load_gx(0, 1, 4)
        load_cs_x()
        load_w(0, 0)
        load_gx(0, 0, 1)
        load_x(0)
        mul_x(0, 2)
        t_w(0, 0, 0)
        load_gm(0, 0)
        t_w(0, 0, 1)
        il_x(0, 0, "s")
        mul_x(0, 3)
        load_gm(0, 1)
        sum_m(0, 3)
        load_x(1)
        load_gm(2, 0)
        add_x(0, 2)
        sum_m(0, 0)
        add_x(0, 3)
        il_x(0, 1, "s")
        il_z(0, 1, "s")
        load_gm(2, 1)
        mul_x(0, 0)
        q_tw(0, 0, 0)
        add_x(0, 0)
        q_tw(0, 0, 1)
        mul_x(0, 1)
        il_x(1, 0, "s")
        q_x(0, 1)
        load_cs_m()
        t_z(0, 1)
        load_gx(2, 0, 4)
        add_x(0, 1)
        q_x(0, 0)
        q_tz(0, 1)
        load_gm(1, 1)
        t_z(0, 0)
        mul_m(0, 0)
        v_m(0)
        il_x(1, 1, "g")
        v_m(1)
        q_tz(0, 0)
        q_m(2, 0)
        sum_m(0, 2)
        mul_m(0, 3)
        load_w(2, 1)
        il_z(2, 0, "g")
        q_x(1, 0)
        q_x(1, 1)
        il_z(0, 0, "s")
        load_gm(1, 0)
        t_z(2, 0)
        t_z(2, 1)
        q_z(2, 0)
        add_m(0, 3)
        q_z(0, 1)
        q_tz(2, 1)
        il_z(2, 1, "g")
        mul_m(0, 2)
        q_z(2, 1)
        sum_m(0, 1)
        load_w(1, 0)
        q_m(2, 1)
        load_w(2, 0)
        dw(2, 0, 1, "ss")
        add_m(0, 2)
        dw(2, 0, 2, "ss")
        dw(2, 0, 3, "ss")
        load_gx(1, 0, 4)
        t_w(2, 1, 0)
        q_tz(2, 0)
        load_w(0, 1)
        q_m(0, 1)
        t_w(1, 0, 0)
        mul_m(0, 1)
        t_w(1, 0, 1)
        t_w(2, 0, 1)
        t_w(2, 0, 0)
        dw(2, 1, 3, "ss")
        dw(0, 1, 0, "ss")
        dw(0, 1, 1, "ss")
        load_w(1, 1)
        dw(2, 1, 1, "ss")
        q_tw(1, 0, 1)
        q_z(0, 0)
        sum_m(1, 2)
        t_w(0, 1, 0)
        add_m(0, 1)
        add_m(0, 0)
        mul_x(1, 2)
        q_m(0, 0)
        mul_x(1, 1)
        t_w(2, 1, 1)
        dw(0, 1, 3, "ss")
        q_tw(1, 0, 0)
        dw(0, 0, 2, "ss")
        dw(0, 0, 3, "ss")
        sum_m(1, 3)
        add_x(1, 2)
        q_tw(2, 0, 1)
        add_x(1, 1)
        dw(0, 1, 2, "ss")
        dw(2, 0, 0, "ss")
        dw(0, 0, 1, "ss")
        dw(0, 0, 0, "ss")
        dw(2, 1, 0, "ss")
        mul_m(1, 2)
        sum_m(1, 0)
        mul_x(1, 0)
        add_x(1, 0)
        mul_x(1, 3)
        q_tw(2, 0, 0)
        t_w(1, 1, 1)
        add_x(1, 3)
        t_w(1, 1, 0)
        q_tw(0, 1, 0)
        t_z(1, 0)
        t_z(1, 1)
        mul_m(1, 3)
        q_tz(1, 1)
        q_tw(2, 1, 1)
        t_w(0, 1, 1)
        q_tz(1, 0)
        sum_m(1, 1)
        q_tw(1, 1, 0)
        q_tw(1, 1, 1)
        q_tw(0, 1, 1)
        dw(2, 1, 2, "ss")
        add_m(1, 2)
        il_z(1, 1, "s")
        il_z(1, 0, "s")
        q_tw(2, 1, 0)
        add_m(1, 3)
        q_m(1, 1)
        q_z(1, 1)
        dx(0, 0, "v")
        mul_m(1, 1)
        dx(1, 0, "s")
        dx(0, 1, "s")
        mul_m(1, 0)
        add_m(1, 0)
        add_m(1, 1)
        dx(1, 1, "s")
        dw(1, 1, 0, "ss")
        dw(1, 1, 1, "ss")
        dw(1, 1, 2, "vs")
        dx(3, 0, "s")
        dw(1, 1, 3, "sv")
        q_m(1, 0)
        q_z(1, 0)
        dx(3, 1, "v")
        dw(1, 0, 3, "ss")
        dw(1, 0, 1, "vs")
        dw(1, 0, 2, "vv")
        dx(2, 0, "s")
        dx(2, 1, "s")
        dw(1, 0, 0, "ss")
